import numpy as np
import ml_dtypes

BF16 = ml_dtypes.bfloat16


def bf(x):
    return np.asarray(x, np.float32).astype(BF16)


def f32(x):
    return np.asarray(x, np.float32)


def f64(x):
    return np.asarray(x).astype(np.float64)


def striped(idx):
    return np.tile(idx.reshape(-1, 16).T, (8, 1))


D, HALF, C, S, N, B, L, WINDOW = 128, 64, 256, 1024, 256, 2, 128, 64
THETA = 10000.0


def rot(a):
    return np.concatenate([-a[HALF:], a[:HALF]], axis=0)


def setup_inputs():
    inv = THETA ** (-np.arange(HALF) / HALF)
    ang = np.outer(inv, S * np.random.random(S))
    ang = np.concatenate([ang, ang], axis=0)
    cs = f32(np.concatenate([np.cos(ang), np.sin(ang)], axis=0))
    q = f32(np.random.standard_normal((D, N)))
    k = f32(np.random.standard_normal((D, N)))
    v = bf(np.random.standard_normal((N, D)))
    return {"cs": cs, "q": q, "k": k, "v": v, "offs": striped(np.random.permutation(np.tile(np.arange(S), 2))[:N])}


def reference(cs, q, k, v, offs):
    idx = offs[:16].T.reshape(-1)
    co = f64(cs)[:D, idx]
    si = f64(cs)[D:, idx]
    qr = f64(q) * co + rot(f64(q)) * si
    kr = f64(k) * co + rot(f64(k)) * si
    u = np.arange(L)[:, None]
    t = np.arange(L)[None, :]
    mask = (t <= u) & (u - t <= WINDOW)
    vv = f64(v)
    res = np.zeros((D, N))
    for b in range(B):
        sl = slice(b * L, (b + 1) * L)
        sc = qr[:, sl].T @ kr[:, sl] / np.sqrt(D)
        e = np.where(mask, np.exp(sc), 0.0)
        p = e / e.sum(axis=1, keepdims=True)
        res[:, sl] = (p @ vv[sl]).T
    return res

@@ -1,0 +1,115 @@
+import math
+
+import concourse.mybir as mybir
+from concourse.masks import make_identity
+
+F32 = mybir.dt.float32
+BF16 = mybir.dt.bfloat16
+U16 = mybir.dt.uint16
+ALU = mybir.AluOpType
+FUNC = mybir.ActivationFunctionType
+
+D = 128
+HALF = D // 2
+POSITIONS = 1024
+TOKENS = 256
+SEQS = 2
+SEQ_LEN = TOKENS // SEQS
+WINDOW = 64
+SCALE = 1.0 / math.sqrt(D)
+MASKED = -1.0e30
+
+FLOPS = SEQS * 2 * (2 * SEQ_LEN * SEQ_LEN * D)
+
+
+def tile_unpaddedmistralattention_kernel(tc, cs, q, k, v, offs, out):
+    nc = tc.nc
+    with (
+        tc.tile_pool(name="held", bufs=1) as held,
+        tc.psum_pool(name="psum", bufs=1) as psum,
+    ):
+        offsets = held.tile([128, TOKENS // 16], U16, name="offsets")
+        nc.sync.dma_start(offsets[:], offs)
+        cos_table = held.tile([D, POSITIONS], F32, name="cos_table")
+        nc.sync.dma_start(cos_table[:], cs[0:D, :])
+        sin_table = held.tile([D, POSITIONS], F32, name="sin_table")
+        nc.sync.dma_start(sin_table[:], cs[D : 2 * D, :])
+
+        plain = {}
+        rotated = {}
+        for name, source in (("q", q), ("k", k)):
+            plain[name] = held.tile([D, TOKENS], F32, name="plain_" + name)
+            nc.scalar.dma_start(plain[name][:], source)
+        for name, source in (("q", q), ("k", k)):
+            rotated[name] = held.tile([D, TOKENS], F32, name="rotated_" + name)
+            nc.scalar.dma_start(rotated[name][0:HALF, :], source[HALF:D, :])
+            nc.scalar.dma_start(rotated[name][HALF:D, :], source[0:HALF, :])
+            nc.scalar.mul(rotated[name][0:HALF, :], rotated[name][0:HALF, :], -1.0)
+
+        values = held.tile([SEQ_LEN, SEQS, D], BF16, name="values")
+        nc.gpsimd.dma_start(values[:], v.rearrange("(s t) d -> t s d", s=SEQS))
+
+        identity = held.tile([128, 128], BF16, name="identity")
+        make_identity(nc, identity[:])
+        distance = held.tile([SEQ_LEN, SEQS, SEQ_LEN], mybir.dt.int32, name="distance")
+        nc.gpsimd.iota(distance[:], pattern=[[0, SEQS], [-1, SEQ_LEN]], base=0, channel_multiplier=1)
+        too_new = held.tile([SEQ_LEN, SEQS, SEQ_LEN], F32, name="too_new")
+        nc.vector.tensor_scalar(too_new[:], distance[:], 0, MASKED, op0=ALU.is_lt, op1=ALU.mult)
+        too_old = held.tile([SEQ_LEN, SEQS, SEQ_LEN], F32, name="too_old")
+        nc.vector.tensor_scalar(too_old[:], distance[:], WINDOW, MASKED, op0=ALU.is_gt, op1=ALU.mult)
+        mask = held.tile([SEQ_LEN, SEQS, SEQ_LEN], BF16, name="mask")
+        nc.vector.tensor_tensor(mask[:], too_new[:], too_old[:], ALU.add)
+
+        roped = {}
+        cos_part = {}
+        sin_part = {}
+        for name in ("q", "k"):
+            cos_part[name] = held.tile([D, TOKENS], F32, name="cos_part_" + name)
+            nc.vector.tensor_tensor(
+                cos_part[name][:], cos_table[:].indirect(offsets[:]), plain[name][:], ALU.mult
+            )
+        for name in ("q", "k"):
+            sin_part[name] = held.tile([D, TOKENS], F32, name="sin_part_" + name)
+            nc.vector.tensor_tensor(
+                sin_part[name][:], sin_table[:].indirect(offsets[:]), rotated[name][:], ALU.mult
+            )
+            roped[name] = held.tile([D, TOKENS], BF16, name="roped_" + name)
+            nc.vector.tensor_tensor(roped[name][:], cos_part[name][:], sin_part[name][:], ALU.add)
+
+        scores = psum.tile([SEQ_LEN, SEQS, SEQ_LEN], F32, name="scores")
+        nc.tensor.matmul(scores[:], lhsT=identity[:], rhs=mask[:], start=True, stop=False)
+        for s in range(SEQS):
+            tokens = slice(s * SEQ_LEN, (s + 1) * SEQ_LEN)
+            nc.tensor.matmul(
+                scores[:, s, :], lhsT=roped["q"][:, tokens], rhs=roped["k"][:, tokens],
+                start=False, stop=(s == SEQS - 1),
+            )
+
+        neg_max = held.tile([SEQ_LEN, SEQS], F32, name="neg_max")
+        nc.vector.tensor_reduce(neg_max[:], scores[:], axis=mybir.AxisListType.X, op=ALU.max, negate=True)
+        shift = held.tile([SEQ_LEN, SEQS], F32, name="shift")
+        nc.vector.tensor_scalar(shift[:], neg_max[:], SCALE, None, op0=ALU.mult)
+        exps = held.tile([SEQ_LEN, SEQS, SEQ_LEN], F32, name="exps")
+        row_sum = held.tile([SEQ_LEN, SEQS], F32, name="row_sum")
+        for s in range(SEQS):
+            nc.scalar.activation(
+                exps[:, s, :], scores[:, s, :], FUNC.Exp,
+                bias=shift[:, s : s + 1], scale=SCALE, accum_out=row_sum[:, s : s + 1],
+            )
+        inv_sum = held.tile([SEQ_LEN, SEQS], F32, name="inv_sum")
+        nc.vector.reciprocal(inv_sum[:], row_sum[:])
+        weights = held.tile([SEQ_LEN, SEQS, SEQ_LEN], BF16, name="weights")
+        for s in range(SEQS):
+            nc.vector.tensor_scalar(weights[:, s, :], exps[:, s, :], inv_sum[:, s : s + 1], None, op0=ALU.mult)
+
+        flipped_psum = psum.tile([SEQ_LEN, SEQS, SEQ_LEN], BF16, name="flipped_psum")
+        for s in range(SEQS):
+            nc.tensor.transpose(flipped_psum[:, s, :], weights[:, s, :], identity[:])
+        flipped = held.tile([SEQ_LEN, SEQS, SEQ_LEN], BF16, name="flipped")
+        nc.vector.tensor_copy(flipped[:], flipped_psum[:])
+        result_psum = psum.tile([D, SEQS, SEQ_LEN], F32, name="result_psum")
+        for s in range(SEQS):
+            nc.tensor.matmul(result_psum[:, s, :], lhsT=values[:, s, :], rhs=flipped[:, s, :], start=True, stop=True)
+        result = held.tile([D, TOKENS], F32, name="result")
+        nc.vector.tensor_copy(result[:], result_psum[:].rearrange("d s j -> d (s j)"))
+        nc.sync.dma_start(out, result[:])

@@ -6,6 +6,7 @@ from concourse.masks import make_identity
 F32 = mybir.dt.float32
 BF16 = mybir.dt.bfloat16
 U16 = mybir.dt.uint16
+I32 = mybir.dt.int32
 ALU = mybir.AluOpType
 FUNC = mybir.ActivationFunctionType
 
@@ -18,6 +19,7 @@ SEQ_LEN = TOKENS // SEQS
 WINDOW = 64
 SCALE = 1.0 / math.sqrt(D)
 MASKED = -1.0e30
+Q, K = 0, 1
 
 FLOPS = SEQS * 2 * (2 * SEQ_LEN * SEQ_LEN * D)
 
@@ -29,87 +31,95 @@ def tile_unpaddedmistralattention_kernel(tc, cs, q, k, v, offs, out):
         tc.psum_pool(name="psum", bufs=1) as psum,
     ):
         offsets = held.tile([128, TOKENS // 16], U16, name="offsets")
-        nc.sync.dma_start(offsets[:], offs)
         cos_table = held.tile([D, POSITIONS], F32, name="cos_table")
-        nc.sync.dma_start(cos_table[:], cs[0:D, :])
         sin_table = held.tile([D, POSITIONS], F32, name="sin_table")
-        nc.sync.dma_start(sin_table[:], cs[D : 2 * D, :])
-
-        plain = {}
-        rotated = {}
-        for name, source in (("q", q), ("k", k)):
-            plain[name] = held.tile([D, TOKENS], F32, name="plain_" + name)
-            nc.scalar.dma_start(plain[name][:], source)
-        for name, source in (("q", q), ("k", k)):
-            rotated[name] = held.tile([D, TOKENS], F32, name="rotated_" + name)
-            nc.scalar.dma_start(rotated[name][0:HALF, :], source[HALF:D, :])
-            nc.scalar.dma_start(rotated[name][HALF:D, :], source[0:HALF, :])
-            nc.scalar.mul(rotated[name][0:HALF, :], rotated[name][0:HALF, :], -1.0)
-
+        plain = held.tile([D, 2, TOKENS], F32, name="plain")
+        rotated = held.tile([D, 2, TOKENS], F32, name="rotated")
         values = held.tile([SEQ_LEN, SEQS, D], BF16, name="values")
-        nc.gpsimd.dma_start(values[:], v.rearrange("(s t) d -> t s d", s=SEQS))
 
-        identity = held.tile([128, 128], BF16, name="identity")
-        make_identity(nc, identity[:])
-        distance = held.tile([SEQ_LEN, SEQS, SEQ_LEN], mybir.dt.int32, name="distance")
-        nc.gpsimd.iota(distance[:], pattern=[[0, SEQS], [-1, SEQ_LEN]], base=0, channel_multiplier=1)
-        too_new = held.tile([SEQ_LEN, SEQS, SEQ_LEN], F32, name="too_new")
+        def load_swapped(which, source):
+            nc.sync.dma_start(rotated[0:HALF, which, :], source[HALF:D, :])
+            nc.sync.dma_start(rotated[HALF:D, which, :], source[0:HALF, :])
+
+        nc.sync.dma_start(offsets[:], offs)
+        nc.scalar.dma_start(plain[:, Q, :], q)
+        nc.scalar.dma_start(plain[:, K, :], k)
+        nc.sync.dma_start(cos_table[:], cs[0:D, :])
+        load_swapped(Q, q)
+        nc.sync.dma_start(sin_table[:], cs[D : 2 * D, :])
+        load_swapped(K, k)
+        nc.sync.dma_start(values[:], v.rearrange("(s t) d -> t s d", s=SEQS))
+
+        warm = held.tile([128, 1], F32, name="warm")
+        nc.vector.memset(warm[:], 0.0)
+        nc.scalar.activation(warm[:], warm[:], FUNC.Exp)
+
+        distance = held.tile([SEQ_LEN, SEQ_LEN], I32, name="distance")
+        nc.gpsimd.iota(distance[:], pattern=[[-1, SEQ_LEN]], base=0, channel_multiplier=1)
+        too_new = held.tile([SEQ_LEN, SEQ_LEN], F32, name="too_new")
         nc.vector.tensor_scalar(too_new[:], distance[:], 0, MASKED, op0=ALU.is_lt, op1=ALU.mult)
-        too_old = held.tile([SEQ_LEN, SEQS, SEQ_LEN], F32, name="too_old")
+        too_old = held.tile([SEQ_LEN, SEQ_LEN], F32, name="too_old")
         nc.vector.tensor_scalar(too_old[:], distance[:], WINDOW, MASKED, op0=ALU.is_gt, op1=ALU.mult)
-        mask = held.tile([SEQ_LEN, SEQS, SEQ_LEN], BF16, name="mask")
+        mask = held.tile([SEQ_LEN, SEQ_LEN], BF16, name="mask")
         nc.vector.tensor_tensor(mask[:], too_new[:], too_old[:], ALU.add)
+        identity = held.tile([128, 128], BF16, name="identity")
+        nc.vector.memset(identity[:], 0.0)
+        make_identity(nc, identity[:], nomemset=True)
 
-        roped = {}
-        cos_part = {}
-        sin_part = {}
-        for name in ("q", "k"):
-            cos_part[name] = held.tile([D, TOKENS], F32, name="cos_part_" + name)
-            nc.vector.tensor_tensor(
-                cos_part[name][:], cos_table[:].indirect(offsets[:]), plain[name][:], ALU.mult
-            )
-        for name in ("q", "k"):
-            sin_part[name] = held.tile([D, TOKENS], F32, name="sin_part_" + name)
-            nc.vector.tensor_tensor(
-                sin_part[name][:], sin_table[:].indirect(offsets[:]), rotated[name][:], ALU.mult
-            )
-            roped[name] = held.tile([D, TOKENS], BF16, name="roped_" + name)
-            nc.vector.tensor_tensor(roped[name][:], cos_part[name][:], sin_part[name][:], ALU.add)
-
-        scores = psum.tile([SEQ_LEN, SEQS, SEQ_LEN], F32, name="scores")
-        nc.tensor.matmul(scores[:], lhsT=identity[:], rhs=mask[:], start=True, stop=False)
+        scores = [psum.tile([SEQ_LEN, SEQ_LEN], F32, name=f"scores{s}") for s in range(SEQS)]
         for s in range(SEQS):
-            tokens = slice(s * SEQ_LEN, (s + 1) * SEQ_LEN)
-            nc.tensor.matmul(
-                scores[:, s, :], lhsT=roped["q"][:, tokens], rhs=roped["k"][:, tokens],
-                start=False, stop=(s == SEQS - 1),
+            nc.tensor.matmul(scores[s][:], lhsT=identity[:], rhs=mask[:], start=True, stop=False)
+
+        cos_part = held.tile([D, 2, TOKENS], F32, name="cos_part")
+        sin_part = held.tile([D, 2, TOKENS], F32, name="sin_part")
+        for which in (Q, K):
+            nc.vector.tensor_tensor(
+                cos_part[:, which, :], cos_table[:].indirect(offsets[:]), plain[:, which, :], ALU.mult
             )
+        for which in (Q, K):
+            nc.scalar.mul(rotated[0:HALF, which, :], rotated[0:HALF, which, :], -1.0)
+            nc.vector.tensor_tensor(
+                sin_part[:, which, :], sin_table[:].indirect(offsets[:]), rotated[:, which, :], ALU.mult
+            )
+        roped = held.tile([D, 2, TOKENS], BF16, name="roped")
+        spans = [slice(s * SEQ_LEN, (s + 1) * SEQ_LEN) for s in range(SEQS)]
+        for s in range(SEQS):
+            nc.vector.tensor_tensor(roped[:, :, spans[s]], cos_part[:, :, spans[s]], sin_part[:, :, spans[s]], ALU.add)
 
         neg_max = held.tile([SEQ_LEN, SEQS], F32, name="neg_max")
-        nc.vector.tensor_reduce(neg_max[:], scores[:], axis=mybir.AxisListType.X, op=ALU.max, negate=True)
         shift = held.tile([SEQ_LEN, SEQS], F32, name="shift")
-        nc.vector.tensor_scalar(shift[:], neg_max[:], SCALE, None, op0=ALU.mult)
-        exps = held.tile([SEQ_LEN, SEQS, SEQ_LEN], F32, name="exps")
         row_sum = held.tile([SEQ_LEN, SEQS], F32, name="row_sum")
+        inv_sum = held.tile([SEQ_LEN, SEQS], F32, name="inv_sum")
+        exps = held.tile([SEQ_LEN, SEQS, SEQ_LEN], F32, name="exps")
+        weights = held.tile([SEQ_LEN, SEQS, SEQ_LEN], BF16, name="weights")
+        flipped = held.tile([SEQ_LEN, SEQS, SEQ_LEN], BF16, name="flipped")
+        result = held.tile([D, TOKENS], F32, name="result")
+        flipped_psum = [psum.tile([SEQ_LEN, SEQ_LEN], BF16, name=f"flipped_psum{s}") for s in range(SEQS)]
+        result_psum = [psum.tile([D, SEQ_LEN], F32, name=f"result_psum{s}") for s in range(SEQS)]
+
+        for s in range(SEQS):
+            nc.tensor.matmul(
+                scores[s][:], lhsT=roped[:, Q, spans[s]], rhs=roped[:, K, spans[s]], start=False, stop=True
+            )
+        for s in range(SEQS):
+            nc.vector.tensor_reduce(
+                neg_max[:, s : s + 1], scores[s][:], axis=mybir.AxisListType.X, op=ALU.max, negate=True
+            )
+            nc.vector.tensor_scalar(shift[:, s : s + 1], neg_max[:, s : s + 1], SCALE, None, op0=ALU.mult)
         for s in range(SEQS):
             nc.scalar.activation(
-                exps[:, s, :], scores[:, s, :], FUNC.Exp,
+                exps[:, s, :], scores[s][:], FUNC.Exp,
                 bias=shift[:, s : s + 1], scale=SCALE, accum_out=row_sum[:, s : s + 1],
             )
-        inv_sum = held.tile([SEQ_LEN, SEQS], F32, name="inv_sum")
-        nc.vector.reciprocal(inv_sum[:], row_sum[:])
-        weights = held.tile([SEQ_LEN, SEQS, SEQ_LEN], BF16, name="weights")
         for s in range(SEQS):
+            nc.vector.reciprocal(inv_sum[:, s : s + 1], row_sum[:, s : s + 1])
             nc.vector.tensor_scalar(weights[:, s, :], exps[:, s, :], inv_sum[:, s : s + 1], None, op0=ALU.mult)
-
-        flipped_psum = psum.tile([SEQ_LEN, SEQS, SEQ_LEN], BF16, name="flipped_psum")
         for s in range(SEQS):
-            nc.tensor.transpose(flipped_psum[:, s, :], weights[:, s, :], identity[:])
-        flipped = held.tile([SEQ_LEN, SEQS, SEQ_LEN], BF16, name="flipped")
-        nc.vector.tensor_copy(flipped[:], flipped_psum[:])
-        result_psum = psum.tile([D, SEQS, SEQ_LEN], F32, name="result_psum")
+            nc.tensor.transpose(flipped_psum[s][:], weights[:, s, :], identity[:])
         for s in range(SEQS):
-            nc.tensor.matmul(result_psum[:, s, :], lhsT=values[:, s, :], rhs=flipped[:, s, :], start=True, stop=True)
-        result = held.tile([D, TOKENS], F32, name="result")
-        nc.vector.tensor_copy(result[:], result_psum[:].rearrange("d s j -> d (s j)"))
-        nc.sync.dma_start(out, result[:])
+            nc.scalar.copy(flipped[:, s, :], flipped_psum[s][:])
+        for s in range(SEQS):
+            nc.tensor.matmul(result_psum[s][:], lhsT=values[:, s, :], rhs=flipped[:, s, :], start=True, stop=True)
+        for s in range(SEQS):
+            nc.scalar.copy(result[:, spans[s]], result_psum[s][:])
+            nc.sync.dma_start(out[:, spans[s]], result[:, spans[s]])

@@ -37,17 +37,11 @@ def tile_unpaddedmistralattention_kernel(tc, cs, q, k, v, offs, out):
         rotated = held.tile([D, 2, TOKENS], F32, name="rotated")
         values = held.tile([SEQ_LEN, SEQS, D], BF16, name="values")
 
-        def load_swapped(which, source):
-            nc.sync.dma_start(rotated[0:HALF, which, :], source[HALF:D, :])
-            nc.sync.dma_start(rotated[HALF:D, which, :], source[0:HALF, :])
-
         nc.sync.dma_start(offsets[:], offs)
         nc.scalar.dma_start(plain[:, Q, :], q)
         nc.scalar.dma_start(plain[:, K, :], k)
         nc.sync.dma_start(cos_table[:], cs[0:D, :])
-        load_swapped(Q, q)
         nc.sync.dma_start(sin_table[:], cs[D : 2 * D, :])
-        load_swapped(K, k)
         nc.sync.dma_start(values[:], v.rearrange("(s t) d -> t s d", s=SEQS))
 
         warm = held.tile([128, 1], F32, name="warm")
@@ -66,6 +60,14 @@ def tile_unpaddedmistralattention_kernel(tc, cs, q, k, v, offs, out):
         nc.vector.memset(identity[:], 0.0)
         make_identity(nc, identity[:], nomemset=True)
 
+        turn = held.tile([D, D], F32, name="turn")
+        nc.vector.tensor_scalar(turn[:, 0:HALF], identity[:, HALF:D], -1.0, None, op0=ALU.mult)
+        nc.vector.tensor_copy(turn[:, HALF:D], identity[:, 0:HALF])
+        rotated_psum = [psum.tile([D, TOKENS], F32, name=f"rotated_psum{which}") for which in (Q, K)]
+        for which in (Q, K):
+            nc.tensor.matmul(rotated_psum[which][:], lhsT=turn[:], rhs=plain[:, which, :], start=True, stop=True)
+            nc.scalar.copy(rotated[:, which, :], rotated_psum[which][:])
+
         scores = [psum.tile([SEQ_LEN, SEQ_LEN], F32, name=f"scores{s}") for s in range(SEQS)]
         for s in range(SEQS):
             nc.tensor.matmul(scores[s][:], lhsT=identity[:], rhs=mask[:], start=True, stop=False)
@@ -77,7 +79,6 @@ def tile_unpaddedmistralattention_kernel(tc, cs, q, k, v, offs, out):
                 cos_part[:, which, :], cos_table[:].indirect(offsets[:]), plain[:, which, :], ALU.mult
             )
         for which in (Q, K):
-            nc.scalar.mul(rotated[0:HALF, which, :], rotated[0:HALF, which, :], -1.0)
             nc.vector.tensor_tensor(
                 sin_part[:, which, :], sin_table[:].indirect(offsets[:]), rotated[:, which, :], ALU.mult
             )

@@ -33,40 +33,46 @@ def tile_unpaddedmistralattention_kernel(tc, cs, q, k, v, offs, out):
         offsets = held.tile([128, TOKENS // 16], U16, name="offsets")
         cos_table = held.tile([D, POSITIONS], F32, name="cos_table")
         sin_table = held.tile([D, POSITIONS], F32, name="sin_table")
-        plain = held.tile([D, 2, TOKENS], F32, name="plain")
-        rotated = held.tile([D, 2, TOKENS], F32, name="rotated")
+        loaded = held.tile([D, 2, TOKENS], F32, name="loaded")
         values = held.tile([SEQ_LEN, SEQS, D], BF16, name="values")
 
         nc.sync.dma_start(offsets[:], offs)
-        nc.scalar.dma_start(plain[:, Q, :], q)
-        nc.scalar.dma_start(plain[:, K, :], k)
+        nc.scalar.dma_start(loaded[:, Q, :], q)
+        nc.scalar.dma_start(loaded[:, K, :], k)
         nc.sync.dma_start(cos_table[:], cs[0:D, :])
         nc.sync.dma_start(sin_table[:], cs[D : 2 * D, :])
         nc.sync.dma_start(values[:], v.rearrange("(s t) d -> t s d", s=SEQS))
 
         warm = held.tile([128, 1], F32, name="warm")
-        nc.vector.memset(warm[:], 0.0)
+        nc.gpsimd.memset(warm[:], 0.0)
         nc.scalar.activation(warm[:], warm[:], FUNC.Exp)
 
-        distance = held.tile([SEQ_LEN, SEQ_LEN], I32, name="distance")
-        nc.gpsimd.iota(distance[:], pattern=[[-1, SEQ_LEN]], base=0, channel_multiplier=1)
-        too_new = held.tile([SEQ_LEN, SEQ_LEN], F32, name="too_new")
-        nc.vector.tensor_scalar(too_new[:], distance[:], 0, MASKED, op0=ALU.is_lt, op1=ALU.mult)
-        too_old = held.tile([SEQ_LEN, SEQ_LEN], F32, name="too_old")
-        nc.vector.tensor_scalar(too_old[:], distance[:], WINDOW, MASKED, op0=ALU.is_gt, op1=ALU.mult)
-        mask = held.tile([SEQ_LEN, SEQ_LEN], BF16, name="mask")
-        nc.vector.tensor_tensor(mask[:], too_new[:], too_old[:], ALU.add)
         identity = held.tile([128, 128], BF16, name="identity")
-        nc.vector.memset(identity[:], 0.0)
-        make_identity(nc, identity[:], nomemset=True)
-
+        make_identity(nc, identity[:])
         turn = held.tile([D, D], F32, name="turn")
-        nc.vector.tensor_scalar(turn[:, 0:HALF], identity[:, HALF:D], -1.0, None, op0=ALU.mult)
-        nc.vector.tensor_copy(turn[:, HALF:D], identity[:, 0:HALF])
+        nc.gpsimd.tensor_scalar(turn[:, 0:HALF], identity[:, HALF:D], -1.0, None, op0=ALU.mult)
+        nc.gpsimd.tensor_copy(turn[:, HALF:D], identity[:, 0:HALF])
+        distance = held.tile([SEQ_LEN, SEQ_LEN], F32, name="distance")
+        nc.gpsimd.iota(
+            distance[:], pattern=[[-1, SEQ_LEN]], base=0, channel_multiplier=1,
+            allow_small_or_imprecise_dtypes=True,
+        )
+        too_new = held.tile([SEQ_LEN, SEQ_LEN], F32, name="too_new")
+        nc.gpsimd.tensor_scalar(too_new[:], distance[:], 0.0, MASKED, op0=ALU.is_lt, op1=ALU.mult)
+        too_old = held.tile([SEQ_LEN, SEQ_LEN], F32, name="too_old")
+        nc.gpsimd.tensor_scalar(too_old[:], distance[:], float(WINDOW), MASKED, op0=ALU.is_gt, op1=ALU.mult)
+        mask = held.tile([SEQ_LEN, SEQ_LEN], BF16, name="mask")
+        nc.gpsimd.tensor_tensor(mask[:], too_new[:], too_old[:], ALU.add)
+
+        scaled_q = held.tile([D, TOKENS], F32, name="scaled_q")
+        nc.scalar.mul(scaled_q[:], loaded[:, Q, :], SCALE)
+        straight = (scaled_q[:], loaded[:, K, :])
+        share = (SCALE, 1.0)
+        rotated = held.tile([D, 2, TOKENS], F32, name="rotated")
         rotated_psum = [psum.tile([D, TOKENS], F32, name=f"rotated_psum{which}") for which in (Q, K)]
         for which in (Q, K):
-            nc.tensor.matmul(rotated_psum[which][:], lhsT=turn[:], rhs=plain[:, which, :], start=True, stop=True)
-            nc.scalar.copy(rotated[:, which, :], rotated_psum[which][:])
+            nc.tensor.matmul(rotated_psum[which][:], lhsT=turn[:], rhs=loaded[:, which, :], start=True, stop=True)
+            nc.scalar.mul(rotated[:, which, :], rotated_psum[which][:], share[which])
 
         scores = [psum.tile([SEQ_LEN, SEQ_LEN], F32, name=f"scores{s}") for s in range(SEQS)]
         for s in range(SEQS):
@@ -74,21 +80,23 @@ def tile_unpaddedmistralattention_kernel(tc, cs, q, k, v, offs, out):
 
         cos_part = held.tile([D, 2, TOKENS], F32, name="cos_part")
         sin_part = held.tile([D, 2, TOKENS], F32, name="sin_part")
-        for which in (Q, K):
-            nc.vector.tensor_tensor(
-                cos_part[:, which, :], cos_table[:].indirect(offsets[:]), plain[:, which, :], ALU.mult
-            )
-        for which in (Q, K):
-            nc.vector.tensor_tensor(
-                sin_part[:, which, :], sin_table[:].indirect(offsets[:]), rotated[:, which, :], ALU.mult
-            )
         roped = held.tile([D, 2, TOKENS], BF16, name="roped")
         spans = [slice(s * SEQ_LEN, (s + 1) * SEQ_LEN) for s in range(SEQS)]
+        for which in (K, Q):
+            nc.vector.tensor_tensor(
+                cos_part[:, which, :], cos_table[:].indirect(offsets[:]), straight[which], ALU.mult
+            )
+        nc.vector.tensor_tensor(
+            sin_part[:, Q, :], sin_table[:].indirect(offsets[:]), rotated[:, Q, :], ALU.mult
+        )
+        nc.vector.tensor_tensor(roped[:, Q, :], cos_part[:, Q, :], sin_part[:, Q, :], ALU.add)
+        nc.vector.tensor_tensor(
+            sin_part[:, K, :], sin_table[:].indirect(offsets[:]), rotated[:, K, :], ALU.mult
+        )
         for s in range(SEQS):
-            nc.vector.tensor_tensor(roped[:, :, spans[s]], cos_part[:, :, spans[s]], sin_part[:, :, spans[s]], ALU.add)
+            nc.vector.tensor_tensor(roped[:, K, spans[s]], cos_part[:, K, spans[s]], sin_part[:, K, spans[s]], ALU.add)
 
         neg_max = held.tile([SEQ_LEN, SEQS], F32, name="neg_max")
-        shift = held.tile([SEQ_LEN, SEQS], F32, name="shift")
         row_sum = held.tile([SEQ_LEN, SEQS], F32, name="row_sum")
         inv_sum = held.tile([SEQ_LEN, SEQS], F32, name="inv_sum")
         exps = held.tile([SEQ_LEN, SEQS, SEQ_LEN], F32, name="exps")
@@ -98,6 +106,9 @@ def tile_unpaddedmistralattention_kernel(tc, cs, q, k, v, offs, out):
         flipped_psum = [psum.tile([SEQ_LEN, SEQ_LEN], BF16, name=f"flipped_psum{s}") for s in range(SEQS)]
         result_psum = [psum.tile([D, SEQ_LEN], F32, name=f"result_psum{s}") for s in range(SEQS)]
 
+        copy_out = (nc.scalar.copy, nc.vector.tensor_copy)
+        store = (nc.scalar.dma_start, nc.sync.dma_start)
+
         for s in range(SEQS):
             nc.tensor.matmul(
                 scores[s][:], lhsT=roped[:, Q, spans[s]], rhs=roped[:, K, spans[s]], start=False, stop=True
@@ -106,11 +117,10 @@ def tile_unpaddedmistralattention_kernel(tc, cs, q, k, v, offs, out):
             nc.vector.tensor_reduce(
                 neg_max[:, s : s + 1], scores[s][:], axis=mybir.AxisListType.X, op=ALU.max, negate=True
             )
-            nc.vector.tensor_scalar(shift[:, s : s + 1], neg_max[:, s : s + 1], SCALE, None, op0=ALU.mult)
         for s in range(SEQS):
             nc.scalar.activation(
                 exps[:, s, :], scores[s][:], FUNC.Exp,
-                bias=shift[:, s : s + 1], scale=SCALE, accum_out=row_sum[:, s : s + 1],
+                bias=neg_max[:, s : s + 1], scale=1.0, accum_out=row_sum[:, s : s + 1],
             )
         for s in range(SEQS):
             nc.vector.reciprocal(inv_sum[:, s : s + 1], row_sum[:, s : s + 1])
@@ -118,9 +128,9 @@ def tile_unpaddedmistralattention_kernel(tc, cs, q, k, v, offs, out):
         for s in range(SEQS):
             nc.tensor.transpose(flipped_psum[s][:], weights[:, s, :], identity[:])
         for s in range(SEQS):
-            nc.scalar.copy(flipped[:, s, :], flipped_psum[s][:])
+            copy_out[s](flipped[:, s, :], flipped_psum[s][:])
         for s in range(SEQS):
             nc.tensor.matmul(result_psum[s][:], lhsT=values[:, s, :], rhs=flipped[:, s, :], start=True, stop=True)
         for s in range(SEQS):
-            nc.scalar.copy(result[:, spans[s]], result_psum[s][:])
-            nc.sync.dma_start(out[:, spans[s]], result[:, spans[s]])
+            copy_out[s](result[:, spans[s]], result_psum[s][:])
+            store[s](out[:, spans[s]], result[:, spans[s]])

@@ -89,7 +89,7 @@ def tile_unpaddedmistralattention_kernel(tc, cs, q, k, v, offs, out):
         nc.vector.tensor_tensor(
             sin_part[:, Q, :], sin_table[:].indirect(offsets[:]), rotated[:, Q, :], ALU.mult
         )
-        nc.vector.tensor_tensor(roped[:, Q, :], cos_part[:, Q, :], sin_part[:, Q, :], ALU.add)
+        nc.gpsimd.tensor_tensor(roped[:, Q, :], cos_part[:, Q, :], sin_part[:, Q, :], ALU.add)
         nc.vector.tensor_tensor(
             sin_part[:, K, :], sin_table[:].indirect(offsets[:]), rotated[:, K, :], ALU.mult
         )

@@ -37,18 +37,19 @@ def tile_unpaddedmistralattention_kernel(tc, cs, q, k, v, offs, out):
         values = held.tile([SEQ_LEN, SEQS, D], BF16, name="values")
 
         nc.sync.dma_start(offsets[:], offs)
-        nc.scalar.dma_start(loaded[:, Q, :], q)
+        nc.sync.dma_start(loaded[:, Q, :], q)
         nc.scalar.dma_start(loaded[:, K, :], k)
         nc.sync.dma_start(cos_table[:], cs[0:D, :])
         nc.sync.dma_start(sin_table[:], cs[D : 2 * D, :])
         nc.sync.dma_start(values[:], v.rearrange("(s t) d -> t s d", s=SEQS))
 
         warm = held.tile([128, 1], F32, name="warm")
-        nc.gpsimd.memset(warm[:], 0.0)
+        nc.vector.memset(warm[:], 0.0)
         nc.scalar.activation(warm[:], warm[:], FUNC.Exp)
 
         identity = held.tile([128, 128], BF16, name="identity")
-        make_identity(nc, identity[:])
+        nc.vector.memset(identity[:], 0.0)
+        make_identity(nc, identity[:], nomemset=True)
         turn = held.tile([D, D], F32, name="turn")
         nc.gpsimd.tensor_scalar(turn[:, 0:HALF], identity[:, HALF:D], -1.0, None, op0=ALU.mult)
         nc.gpsimd.tensor_copy(turn[:, HALF:D], identity[:, 0:HALF])
@@ -89,7 +90,7 @@ def tile_unpaddedmistralattention_kernel(tc, cs, q, k, v, offs, out):
         nc.vector.tensor_tensor(
             sin_part[:, Q, :], sin_table[:].indirect(offsets[:]), rotated[:, Q, :], ALU.mult
         )
-        nc.gpsimd.tensor_tensor(roped[:, Q, :], cos_part[:, Q, :], sin_part[:, Q, :], ALU.add)
+        nc.vector.tensor_tensor(roped[:, Q, :], cos_part[:, Q, :], sin_part[:, Q, :], ALU.add)
         nc.vector.tensor_tensor(
             sin_part[:, K, :], sin_table[:].indirect(offsets[:]), rotated[:, K, :], ALU.mult
         )

@@ -36,12 +36,24 @@ def tile_unpaddedmistralattention_kernel(tc, cs, q, k, v, offs, out):
         loaded = held.tile([D, 2, TOKENS], F32, name="loaded")
         values = held.tile([SEQ_LEN, SEQS, D], BF16, name="values")
 
-        nc.sync.dma_start(offsets[:], offs)
         nc.sync.dma_start(loaded[:, Q, :], q)
-        nc.scalar.dma_start(loaded[:, K, :], k)
+        nc.sync.dma_start(loaded[:, K, :], k)
+        nc.sync.dma_start(offsets[:], offs)
         nc.sync.dma_start(cos_table[:], cs[0:D, :])
         nc.sync.dma_start(sin_table[:], cs[D : 2 * D, :])
         nc.sync.dma_start(values[:], v.rearrange("(s t) d -> t s d", s=SEQS))
+
+        swap = held.tile([D, D], F32, name="swap")
+        nc.vector.memset(swap[:], 0.0)
+        nc.gpsimd.affine_select(
+            out=swap[:], in_=swap[:], compare_op=ALU.not_equal, fill=1.0,
+            base=-HALF, channel_multiplier=1, pattern=[[HALF, 2], [-1, HALF]],
+        )
+        share = (SCALE, 1.0)
+        signed_share = held.tile([D, 2], F32, name="signed_share")
+        for which in (Q, K):
+            nc.vector.memset(signed_share[0:HALF, which : which + 1], -share[which])
+            nc.vector.memset(signed_share[HALF:D, which : which + 1], share[which])
 
         warm = held.tile([128, 1], F32, name="warm")
         nc.vector.memset(warm[:], 0.0)
@@ -50,9 +62,6 @@ def tile_unpaddedmistralattention_kernel(tc, cs, q, k, v, offs, out):
         identity = held.tile([128, 128], BF16, name="identity")
         nc.vector.memset(identity[:], 0.0)
         make_identity(nc, identity[:], nomemset=True)
-        turn = held.tile([D, D], F32, name="turn")
-        nc.gpsimd.tensor_scalar(turn[:, 0:HALF], identity[:, HALF:D], -1.0, None, op0=ALU.mult)
-        nc.gpsimd.tensor_copy(turn[:, HALF:D], identity[:, 0:HALF])
         distance = held.tile([SEQ_LEN, SEQ_LEN], F32, name="distance")
         nc.gpsimd.iota(
             distance[:], pattern=[[-1, SEQ_LEN]], base=0, channel_multiplier=1,
@@ -68,12 +77,11 @@ def tile_unpaddedmistralattention_kernel(tc, cs, q, k, v, offs, out):
         scaled_q = held.tile([D, TOKENS], F32, name="scaled_q")
         nc.scalar.mul(scaled_q[:], loaded[:, Q, :], SCALE)
         straight = (scaled_q[:], loaded[:, K, :])
-        share = (SCALE, 1.0)
         rotated = held.tile([D, 2, TOKENS], F32, name="rotated")
-        rotated_psum = [psum.tile([D, TOKENS], F32, name=f"rotated_psum{which}") for which in (Q, K)]
+        swapped_psum = [psum.tile([D, TOKENS], F32, name=f"swapped_psum{which}") for which in (Q, K)]
         for which in (Q, K):
-            nc.tensor.matmul(rotated_psum[which][:], lhsT=turn[:], rhs=loaded[:, which, :], start=True, stop=True)
-            nc.scalar.mul(rotated[:, which, :], rotated_psum[which][:], share[which])
+            nc.tensor.matmul(swapped_psum[which][:], lhsT=swap[:], rhs=loaded[:, which, :], start=True, stop=True)
+            nc.scalar.mul(rotated[:, which, :], swapped_psum[which][:], signed_share[:, which : which + 1])
 
         scores = [psum.tile([SEQ_LEN, SEQ_LEN], F32, name=f"scores{s}") for s in range(SEQS)]
         for s in range(SEQS):

@@ -36,10 +36,10 @@ def tile_unpaddedmistralattention_kernel(tc, cs, q, k, v, offs, out):
         loaded = held.tile([D, 2, TOKENS], F32, name="loaded")
         values = held.tile([SEQ_LEN, SEQS, D], BF16, name="values")
 
-        nc.sync.dma_start(loaded[:, Q, :], q)
-        nc.sync.dma_start(loaded[:, K, :], k)
+        nc.scalar.dma_start(loaded[:, Q, :], q)
         nc.sync.dma_start(offsets[:], offs)
         nc.sync.dma_start(cos_table[:], cs[0:D, :])
+        nc.sync.dma_start(loaded[:, K, :], k)
         nc.sync.dma_start(sin_table[:], cs[D : 2 * D, :])
         nc.sync.dma_start(values[:], v.rearrange("(s t) d -> t s d", s=SEQS))
 
@@ -75,7 +75,7 @@ def tile_unpaddedmistralattention_kernel(tc, cs, q, k, v, offs, out):
         nc.gpsimd.tensor_tensor(mask[:], too_new[:], too_old[:], ALU.add)
 
         scaled_q = held.tile([D, TOKENS], F32, name="scaled_q")
-        nc.scalar.mul(scaled_q[:], loaded[:, Q, :], SCALE)
+        nc.vector.tensor_scalar(scaled_q[:], loaded[:, Q, :], SCALE, None, op0=ALU.mult)
         straight = (scaled_q[:], loaded[:, K, :])
         rotated = held.tile([D, 2, TOKENS], F32, name="rotated")
         swapped_psum = [psum.tile([D, TOKENS], F32, name=f"swapped_psum{which}") for which in (Q, K)]
@@ -91,7 +91,7 @@ def tile_unpaddedmistralattention_kernel(tc, cs, q, k, v, offs, out):
         sin_part = held.tile([D, 2, TOKENS], F32, name="sin_part")
         roped = held.tile([D, 2, TOKENS], BF16, name="roped")
         spans = [slice(s * SEQ_LEN, (s + 1) * SEQ_LEN) for s in range(SEQS)]
-        for which in (K, Q):
+        for which in (Q, K):
             nc.vector.tensor_tensor(
                 cos_part[:, which, :], cos_table[:].indirect(offsets[:]), straight[which], ALU.mult
             )

@@ -37,9 +37,9 @@ def tile_unpaddedmistralattention_kernel(tc, cs, q, k, v, offs, out):
         values = held.tile([SEQ_LEN, SEQS, D], BF16, name="values")
 
         nc.scalar.dma_start(loaded[:, Q, :], q)
-        nc.sync.dma_start(offsets[:], offs)
-        nc.sync.dma_start(cos_table[:], cs[0:D, :])
         nc.sync.dma_start(loaded[:, K, :], k)
+        nc.sync.dma_start(cos_table[:], cs[0:D, :])
+        nc.sync.dma_start(offsets[:], offs)
         nc.sync.dma_start(sin_table[:], cs[D : 2 * D, :])
         nc.sync.dma_start(values[:], v.rearrange("(s t) d -> t s d", s=SEQS))
 

@@ -62,17 +62,16 @@ def tile_unpaddedmistralattention_kernel(tc, cs, q, k, v, offs, out):
         identity = held.tile([128, 128], BF16, name="identity")
         nc.vector.memset(identity[:], 0.0)
         make_identity(nc, identity[:], nomemset=True)
-        distance = held.tile([SEQ_LEN, SEQ_LEN], F32, name="distance")
-        nc.gpsimd.iota(
-            distance[:], pattern=[[-1, SEQ_LEN]], base=0, channel_multiplier=1,
-            allow_small_or_imprecise_dtypes=True,
-        )
-        too_new = held.tile([SEQ_LEN, SEQ_LEN], F32, name="too_new")
-        nc.gpsimd.tensor_scalar(too_new[:], distance[:], 0.0, MASKED, op0=ALU.is_lt, op1=ALU.mult)
-        too_old = held.tile([SEQ_LEN, SEQ_LEN], F32, name="too_old")
-        nc.gpsimd.tensor_scalar(too_old[:], distance[:], float(WINDOW), MASKED, op0=ALU.is_gt, op1=ALU.mult)
         mask = held.tile([SEQ_LEN, SEQ_LEN], BF16, name="mask")
-        nc.gpsimd.tensor_tensor(mask[:], too_new[:], too_old[:], ALU.add)
+        nc.vector.memset(mask[:], 0.0)
+        nc.gpsimd.affine_select(
+            out=mask[:], in_=mask[:], compare_op=ALU.is_ge, fill=MASKED,
+            base=0, channel_multiplier=1, pattern=[[-1, SEQ_LEN]],
+        )
+        nc.gpsimd.affine_select(
+            out=mask[:], in_=mask[:], compare_op=ALU.is_ge, fill=MASKED,
+            base=WINDOW, channel_multiplier=-1, pattern=[[1, SEQ_LEN]],
+        )
 
         scaled_q = held.tile([D, TOKENS], F32, name="scaled_q")
         nc.vector.tensor_scalar(scaled_q[:], loaded[:, Q, :], SCALE, None, op0=ALU.mult)

@@ -36,10 +36,10 @@ def tile_unpaddedmistralattention_kernel(tc, cs, q, k, v, offs, out):
         loaded = held.tile([D, 2, TOKENS], F32, name="loaded")
         values = held.tile([SEQ_LEN, SEQS, D], BF16, name="values")
 
-        nc.scalar.dma_start(loaded[:, Q, :], q)
-        nc.sync.dma_start(loaded[:, K, :], k)
-        nc.sync.dma_start(cos_table[:], cs[0:D, :])
+        nc.sync.dma_start(loaded[:, Q, :], q)
+        nc.scalar.dma_start(cos_table[:], cs[0:D, :])
         nc.sync.dma_start(offsets[:], offs)
+        nc.scalar.dma_start(loaded[:, K, :], k)
         nc.sync.dma_start(sin_table[:], cs[D : 2 * D, :])
         nc.sync.dma_start(values[:], v.rearrange("(s t) d -> t s d", s=SEQS))
 
@@ -76,11 +76,15 @@ def tile_unpaddedmistralattention_kernel(tc, cs, q, k, v, offs, out):
         scaled_q = held.tile([D, TOKENS], F32, name="scaled_q")
         nc.vector.tensor_scalar(scaled_q[:], loaded[:, Q, :], SCALE, None, op0=ALU.mult)
         straight = (scaled_q[:], loaded[:, K, :])
+        spans = [slice(s * SEQ_LEN, (s + 1) * SEQ_LEN) for s in range(SEQS)]
         rotated = held.tile([D, 2, TOKENS], F32, name="rotated")
-        swapped_psum = [psum.tile([D, TOKENS], F32, name=f"swapped_psum{which}") for which in (Q, K)]
-        for which in (Q, K):
-            nc.tensor.matmul(swapped_psum[which][:], lhsT=swap[:], rhs=loaded[:, which, :], start=True, stop=True)
-            nc.scalar.mul(rotated[:, which, :], swapped_psum[which][:], signed_share[:, which : which + 1])
+        swapped_q = psum.tile([D, TOKENS], F32, name="swapped_q")
+        nc.tensor.matmul(swapped_q[:], lhsT=swap[:], rhs=loaded[:, Q, :], start=True, stop=True)
+        nc.scalar.mul(rotated[:, Q, :], swapped_q[:], signed_share[:, Q : Q + 1])
+        swapped_k = [psum.tile([D, SEQ_LEN], F32, name=f"swapped_k{s}") for s in range(SEQS)]
+        for s in range(SEQS):
+            nc.tensor.matmul(swapped_k[s][:], lhsT=swap[:], rhs=loaded[:, K, spans[s]], start=True, stop=True)
+            nc.scalar.mul(rotated[:, K, spans[s]], swapped_k[s][:], signed_share[:, K : K + 1])
 
         scores = [psum.tile([SEQ_LEN, SEQ_LEN], F32, name=f"scores{s}") for s in range(SEQS)]
         for s in range(SEQS):
@@ -89,7 +93,6 @@ def tile_unpaddedmistralattention_kernel(tc, cs, q, k, v, offs, out):
         cos_part = held.tile([D, 2, TOKENS], F32, name="cos_part")
         sin_part = held.tile([D, 2, TOKENS], F32, name="sin_part")
         roped = held.tile([D, 2, TOKENS], BF16, name="roped")
-        spans = [slice(s * SEQ_LEN, (s + 1) * SEQ_LEN) for s in range(SEQS)]
         for which in (Q, K):
             nc.vector.tensor_tensor(
                 cos_part[:, which, :], cos_table[:].indirect(offsets[:]), straight[which], ALU.mult
@@ -98,9 +101,12 @@ def tile_unpaddedmistralattention_kernel(tc, cs, q, k, v, offs, out):
             sin_part[:, Q, :], sin_table[:].indirect(offsets[:]), rotated[:, Q, :], ALU.mult
         )
         nc.vector.tensor_tensor(roped[:, Q, :], cos_part[:, Q, :], sin_part[:, Q, :], ALU.add)
-        nc.vector.tensor_tensor(
-            sin_part[:, K, :], sin_table[:].indirect(offsets[:]), rotated[:, K, :], ALU.mult
-        )
+        list_columns = [slice(s * SEQ_LEN // 16, (s + 1) * SEQ_LEN // 16) for s in range(SEQS)]
+        for s in range(SEQS):
+            nc.vector.tensor_tensor(
+                sin_part[:, K, spans[s]], sin_table[:].indirect(offsets[:, list_columns[s]]),
+                rotated[:, K, spans[s]], ALU.mult,
+            )
         for s in range(SEQS):
             nc.vector.tensor_tensor(roped[:, K, spans[s]], cos_part[:, K, spans[s]], sin_part[:, K, spans[s]], ALU.add)
 
@@ -112,7 +118,7 @@ def tile_unpaddedmistralattention_kernel(tc, cs, q, k, v, offs, out):
         flipped = held.tile([SEQ_LEN, SEQS, SEQ_LEN], BF16, name="flipped")
         result = held.tile([D, TOKENS], F32, name="result")
         flipped_psum = [psum.tile([SEQ_LEN, SEQ_LEN], BF16, name=f"flipped_psum{s}") for s in range(SEQS)]
-        result_psum = [psum.tile([D, SEQ_LEN], F32, name=f"result_psum{s}") for s in range(SEQS)]
+        result_psum = [psum.tile([D, SEQ_LEN], F32, name=f"result_psum{s}", tag=f"swapped_k{s}") for s in range(SEQS)]
 
         copy_out = (nc.scalar.copy, nc.vector.tensor_copy)
         store = (nc.scalar.dma_start, nc.sync.dma_start)

@@ -36,10 +36,10 @@ def tile_unpaddedmistralattention_kernel(tc, cs, q, k, v, offs, out):
         loaded = held.tile([D, 2, TOKENS], F32, name="loaded")
         values = held.tile([SEQ_LEN, SEQS, D], BF16, name="values")
 
-        nc.sync.dma_start(loaded[:, Q, :], q)
-        nc.scalar.dma_start(cos_table[:], cs[0:D, :])
+        nc.scalar.dma_start(loaded[:, Q, :], q)
+        nc.sync.dma_start(loaded[:, K, :], k)
+        nc.sync.dma_start(cos_table[:], cs[0:D, :])
         nc.sync.dma_start(offsets[:], offs)
-        nc.scalar.dma_start(loaded[:, K, :], k)
         nc.sync.dma_start(sin_table[:], cs[D : 2 * D, :])
         nc.sync.dma_start(values[:], v.rearrange("(s t) d -> t s d", s=SEQS))
 

@@ -36,8 +36,8 @@ def tile_unpaddedmistralattention_kernel(tc, cs, q, k, v, offs, out):
         loaded = held.tile([D, 2, TOKENS], F32, name="loaded")
         values = held.tile([SEQ_LEN, SEQS, D], BF16, name="values")
 
-        nc.scalar.dma_start(loaded[:, Q, :], q)
-        nc.sync.dma_start(loaded[:, K, :], k)
+        nc.sync.dma_start(loaded[:, Q, :], q)
+        nc.scalar.dma_start(loaded[:, K, :], k)
         nc.sync.dma_start(cos_table[:], cs[0:D, :])
         nc.sync.dma_start(offsets[:], offs)
         nc.sync.dma_start(sin_table[:], cs[D : 2 * D, :])

@@ -101,12 +101,9 @@ def tile_unpaddedmistralattention_kernel(tc, cs, q, k, v, offs, out):
             sin_part[:, Q, :], sin_table[:].indirect(offsets[:]), rotated[:, Q, :], ALU.mult
         )
         nc.vector.tensor_tensor(roped[:, Q, :], cos_part[:, Q, :], sin_part[:, Q, :], ALU.add)
-        list_columns = [slice(s * SEQ_LEN // 16, (s + 1) * SEQ_LEN // 16) for s in range(SEQS)]
-        for s in range(SEQS):
-            nc.vector.tensor_tensor(
-                sin_part[:, K, spans[s]], sin_table[:].indirect(offsets[:, list_columns[s]]),
-                rotated[:, K, spans[s]], ALU.mult,
-            )
+        nc.vector.tensor_tensor(
+            sin_part[:, K, :], sin_table[:].indirect(offsets[:]), rotated[:, K, :], ALU.mult
+        )
         for s in range(SEQS):
             nc.vector.tensor_tensor(roped[:, K, spans[s]], cos_part[:, K, spans[s]], sin_part[:, K, spans[s]], ALU.add)
 

@@ -62,6 +62,9 @@ def tile_unpaddedmistralattention_kernel(tc, cs, q, k, v, offs, out):
         identity = held.tile([128, 128], BF16, name="identity")
         nc.vector.memset(identity[:], 0.0)
         make_identity(nc, identity[:], nomemset=True)
+        identity_f32 = held.tile([128, 128], F32, name="identity_f32")
+        nc.vector.memset(identity_f32[:], 0.0)
+        make_identity(nc, identity_f32[:], nomemset=True)
         mask = held.tile([SEQ_LEN, SEQ_LEN], BF16, name="mask")
         nc.vector.memset(mask[:], 0.0)
         nc.gpsimd.affine_select(
@@ -93,19 +96,28 @@ def tile_unpaddedmistralattention_kernel(tc, cs, q, k, v, offs, out):
         cos_part = held.tile([D, 2, TOKENS], F32, name="cos_part")
         sin_part = held.tile([D, 2, TOKENS], F32, name="sin_part")
         roped = held.tile([D, 2, TOKENS], BF16, name="roped")
-        for which in (Q, K):
-            nc.vector.tensor_tensor(
-                cos_part[:, which, :], cos_table[:].indirect(offsets[:]), straight[which], ALU.mult
-            )
+        nc.vector.tensor_tensor(
+            cos_part[:, Q, :], cos_table[:].indirect(offsets[:]), straight[Q], ALU.mult
+        )
+        nc.vector.tensor_tensor(
+            cos_part[:, K, :], cos_table[:].indirect(offsets[:]), straight[K], ALU.mult
+        )
         nc.vector.tensor_tensor(
             sin_part[:, Q, :], sin_table[:].indirect(offsets[:]), rotated[:, Q, :], ALU.mult
         )
-        nc.vector.tensor_tensor(roped[:, Q, :], cos_part[:, Q, :], sin_part[:, Q, :], ALU.add)
-        nc.vector.tensor_tensor(
-            sin_part[:, K, :], sin_table[:].indirect(offsets[:]), rotated[:, K, :], ALU.mult
-        )
+        q_sum = psum.tile([D, SEQ_LEN], F32, name="q_sum")
+        nc.tensor.matmul(q_sum[:], lhsT=identity_f32[:], rhs=cos_part[:, Q, spans[1]], start=True, stop=False)
+        nc.tensor.matmul(q_sum[:], lhsT=identity_f32[:], rhs=sin_part[:, Q, spans[1]], start=False, stop=True)
+        nc.scalar.copy(roped[:, Q, spans[1]], q_sum[:])
+        lists = [offsets[:, s * SEQ_LEN // 16 : (s + 1) * SEQ_LEN // 16] for s in range(SEQS)]
         for s in range(SEQS):
-            nc.vector.tensor_tensor(roped[:, K, spans[s]], cos_part[:, K, spans[s]], sin_part[:, K, spans[s]], ALU.add)
+            nc.vector.tensor_tensor(
+                sin_part[:, K, spans[s]], sin_table[:].indirect(lists[s]), rotated[:, K, spans[s]], ALU.mult
+            )
+        for which, s in ((Q, 0), (K, 0), (K, 1)):
+            nc.vector.tensor_tensor(
+                roped[:, which, spans[s]], cos_part[:, which, spans[s]], sin_part[:, which, spans[s]], ALU.add
+            )
 
         neg_max = held.tile([SEQ_LEN, SEQS], F32, name="neg_max")
         row_sum = held.tile([SEQ_LEN, SEQS], F32, name="row_sum")

@@ -89,10 +89,6 @@ def tile_unpaddedmistralattention_kernel(tc, cs, q, k, v, offs, out):
             nc.tensor.matmul(swapped_k[s][:], lhsT=swap[:], rhs=loaded[:, K, spans[s]], start=True, stop=True)
             nc.scalar.mul(rotated[:, K, spans[s]], swapped_k[s][:], signed_share[:, K : K + 1])
 
-        scores = [psum.tile([SEQ_LEN, SEQ_LEN], F32, name=f"scores{s}") for s in range(SEQS)]
-        for s in range(SEQS):
-            nc.tensor.matmul(scores[s][:], lhsT=identity[:], rhs=mask[:], start=True, stop=False)
-
         cos_part = held.tile([D, 2, TOKENS], F32, name="cos_part")
         sin_part = held.tile([D, 2, TOKENS], F32, name="sin_part")
         roped = held.tile([D, 2, TOKENS], BF16, name="roped")
@@ -118,6 +114,10 @@ def tile_unpaddedmistralattention_kernel(tc, cs, q, k, v, offs, out):
             nc.vector.tensor_tensor(
                 roped[:, which, spans[s]], cos_part[:, which, spans[s]], sin_part[:, which, spans[s]], ALU.add
             )
+
+        scores = [psum.tile([SEQ_LEN, SEQ_LEN], F32, name=f"scores{s}") for s in range(SEQS)]
+        for s in range(SEQS):
+            nc.tensor.matmul(scores[s][:], lhsT=identity[:], rhs=mask[:], start=True, stop=False)
 
         neg_max = held.tile([SEQ_LEN, SEQS], F32, name="neg_max")
         row_sum = held.tile([SEQ_LEN, SEQS], F32, name="row_sum")
@@ -149,7 +149,7 @@ def tile_unpaddedmistralattention_kernel(tc, cs, q, k, v, offs, out):
             nc.vector.reciprocal(inv_sum[:, s : s + 1], row_sum[:, s : s + 1])
             nc.vector.tensor_scalar(weights[:, s, :], exps[:, s, :], inv_sum[:, s : s + 1], None, op0=ALU.mult)
         for s in range(SEQS):
-            nc.tensor.transpose(flipped_psum[s][:], weights[:, s, :], identity[:])
+            nc.tensor.matmul(flipped_psum[s][:], lhsT=weights[:, s, :], rhs=identity[:], start=True, stop=True)
         for s in range(SEQS):
             copy_out[s](flipped[:, s, :], flipped_psum[s][:])
         for s in range(SEQS):

import math

import concourse.mybir as mybir
from concourse.masks import make_identity

F32 = mybir.dt.float32
BF16 = mybir.dt.bfloat16
U16 = mybir.dt.uint16
I32 = mybir.dt.int32
ALU = mybir.AluOpType
FUNC = mybir.ActivationFunctionType

D = 128
HALF = D // 2
POSITIONS = 1024
TOKENS = 256
SEQS = 2
SEQ_LEN = TOKENS // SEQS
WINDOW = 64
SCALE = 1.0 / math.sqrt(D)
MASKED = -1.0e30
Q, K = 0, 1

FLOPS = SEQS * 2 * (2 * SEQ_LEN * SEQ_LEN * D)


def tile_unpaddedmistralattention_kernel(tc, cs, q, k, v, offs, out):
    nc = tc.nc
    with (
        tc.tile_pool(name="held", bufs=1) as held,
        tc.psum_pool(name="psum", bufs=1) as psum,
    ):
        offsets = held.tile([128, TOKENS // 16], U16, name="offsets")
        cos_table = held.tile([D, POSITIONS], F32, name="cos_table")
        sin_table = held.tile([D, POSITIONS], F32, name="sin_table")
        loaded = held.tile([D, 2, TOKENS], F32, name="loaded")
        values = held.tile([SEQ_LEN, SEQS, D], BF16, name="values")

        nc.sync.dma_start(loaded[:, Q, :], q)
        nc.scalar.dma_start(loaded[:, K, :], k)
        nc.sync.dma_start(cos_table[:], cs[0:D, :])
        nc.sync.dma_start(offsets[:], offs)
        nc.sync.dma_start(sin_table[:], cs[D : 2 * D, :])
        nc.sync.dma_start(values[:], v.rearrange("(s t) d -> t s d", s=SEQS))

        swap = held.tile([D, D], F32, name="swap")
        nc.vector.memset(swap[:], 0.0)
        nc.gpsimd.affine_select(
            out=swap[:], in_=swap[:], compare_op=ALU.not_equal, fill=1.0,
            base=-HALF, channel_multiplier=1, pattern=[[HALF, 2], [-1, HALF]],
        )
        share = (SCALE, 1.0)
        signed_share = held.tile([D, 2], F32, name="signed_share")
        for which in (Q, K):
            nc.vector.memset(signed_share[0:HALF, which : which + 1], -share[which])
            nc.vector.memset(signed_share[HALF:D, which : which + 1], share[which])

        warm = held.tile([128, 1], F32, name="warm")
        nc.vector.memset(warm[:], 0.0)
        nc.scalar.activation(warm[:], warm[:], FUNC.Exp)

        identity = held.tile([128, 128], BF16, name="identity")
        nc.vector.memset(identity[:], 0.0)
        make_identity(nc, identity[:], nomemset=True)
        identity_f32 = held.tile([128, 128], F32, name="identity_f32")
        nc.vector.memset(identity_f32[:], 0.0)
        make_identity(nc, identity_f32[:], nomemset=True)
        mask = held.tile([SEQ_LEN, SEQ_LEN], BF16, name="mask")
        nc.vector.memset(mask[:], 0.0)
        nc.gpsimd.affine_select(
            out=mask[:], in_=mask[:], compare_op=ALU.is_ge, fill=MASKED,
            base=0, channel_multiplier=1, pattern=[[-1, SEQ_LEN]],
        )
        nc.gpsimd.affine_select(
            out=mask[:], in_=mask[:], compare_op=ALU.is_ge, fill=MASKED,
            base=WINDOW, channel_multiplier=-1, pattern=[[1, SEQ_LEN]],
        )

        scaled_q = held.tile([D, TOKENS], F32, name="scaled_q")
        nc.vector.tensor_scalar(scaled_q[:], loaded[:, Q, :], SCALE, None, op0=ALU.mult)
        straight = (scaled_q[:], loaded[:, K, :])
        spans = [slice(s * SEQ_LEN, (s + 1) * SEQ_LEN) for s in range(SEQS)]
        rotated = held.tile([D, 2, TOKENS], F32, name="rotated")
        swapped_q = psum.tile([D, TOKENS], F32, name="swapped_q")
        nc.tensor.matmul(swapped_q[:], lhsT=swap[:], rhs=loaded[:, Q, :], start=True, stop=True)
        nc.scalar.mul(rotated[:, Q, :], swapped_q[:], signed_share[:, Q : Q + 1])
        swapped_k = [psum.tile([D, SEQ_LEN], F32, name=f"swapped_k{s}") for s in range(SEQS)]
        for s in range(SEQS):
            nc.tensor.matmul(swapped_k[s][:], lhsT=swap[:], rhs=loaded[:, K, spans[s]], start=True, stop=True)
            nc.scalar.mul(rotated[:, K, spans[s]], swapped_k[s][:], signed_share[:, K : K + 1])

        cos_part = held.tile([D, 2, TOKENS], F32, name="cos_part")
        sin_part = held.tile([D, 2, TOKENS], F32, name="sin_part")
        roped = held.tile([D, 2, TOKENS], BF16, name="roped")
        nc.vector.tensor_tensor(
            cos_part[:, Q, :], cos_table[:].indirect(offsets[:]), straight[Q], ALU.mult
        )
        nc.vector.tensor_tensor(
            cos_part[:, K, :], cos_table[:].indirect(offsets[:]), straight[K], ALU.mult
        )
        nc.vector.tensor_tensor(
            sin_part[:, Q, :], sin_table[:].indirect(offsets[:]), rotated[:, Q, :], ALU.mult
        )
        q_sum = psum.tile([D, SEQ_LEN], F32, name="q_sum")
        nc.tensor.matmul(q_sum[:], lhsT=identity_f32[:], rhs=cos_part[:, Q, spans[1]], start=True, stop=False)
        nc.tensor.matmul(q_sum[:], lhsT=identity_f32[:], rhs=sin_part[:, Q, spans[1]], start=False, stop=True)
        nc.scalar.copy(roped[:, Q, spans[1]], q_sum[:])
        lists = [offsets[:, s * SEQ_LEN // 16 : (s + 1) * SEQ_LEN // 16] for s in range(SEQS)]
        for s in range(SEQS):
            nc.vector.tensor_tensor(
                sin_part[:, K, spans[s]], sin_table[:].indirect(lists[s]), rotated[:, K, spans[s]], ALU.mult
            )
        for which, s in ((Q, 0), (K, 0), (K, 1)):
            nc.vector.tensor_tensor(
                roped[:, which, spans[s]], cos_part[:, which, spans[s]], sin_part[:, which, spans[s]], ALU.add
            )

        scores = [psum.tile([SEQ_LEN, SEQ_LEN], F32, name=f"scores{s}") for s in range(SEQS)]
        for s in range(SEQS):
            nc.tensor.matmul(scores[s][:], lhsT=identity[:], rhs=mask[:], start=True, stop=False)

        neg_max = held.tile([SEQ_LEN, SEQS], F32, name="neg_max")
        row_sum = held.tile([SEQ_LEN, SEQS], F32, name="row_sum")
        inv_sum = held.tile([SEQ_LEN, SEQS], F32, name="inv_sum")
        exps = held.tile([SEQ_LEN, SEQS, SEQ_LEN], F32, name="exps")
        weights = held.tile([SEQ_LEN, SEQS, SEQ_LEN], BF16, name="weights")
        flipped = held.tile([SEQ_LEN, SEQS, SEQ_LEN], BF16, name="flipped")
        result = held.tile([D, TOKENS], F32, name="result")
        flipped_psum = [psum.tile([SEQ_LEN, SEQ_LEN], BF16, name=f"flipped_psum{s}") for s in range(SEQS)]
        result_psum = [psum.tile([D, SEQ_LEN], F32, name=f"result_psum{s}", tag=f"swapped_k{s}") for s in range(SEQS)]

        copy_out = (nc.scalar.copy, nc.vector.tensor_copy)
        store = (nc.scalar.dma_start, nc.sync.dma_start)

        for s in range(SEQS):
            nc.tensor.matmul(
                scores[s][:], lhsT=roped[:, Q, spans[s]], rhs=roped[:, K, spans[s]], start=False, stop=True
            )
        for s in range(SEQS):
            nc.vector.tensor_reduce(
                neg_max[:, s : s + 1], scores[s][:], axis=mybir.AxisListType.X, op=ALU.max, negate=True
            )
        for s in range(SEQS):
            nc.scalar.activation(
                exps[:, s, :], scores[s][:], FUNC.Exp,
                bias=neg_max[:, s : s + 1], scale=1.0, accum_out=row_sum[:, s : s + 1],
            )
        for s in range(SEQS):
            nc.vector.reciprocal(inv_sum[:, s : s + 1], row_sum[:, s : s + 1])
            nc.vector.tensor_scalar(weights[:, s, :], exps[:, s, :], inv_sum[:, s : s + 1], None, op0=ALU.mult)
        for s in range(SEQS):
            nc.tensor.matmul(flipped_psum[s][:], lhsT=weights[:, s, :], rhs=identity[:], start=True, stop=True)
        for s in range(SEQS):
            copy_out[s](flipped[:, s, :], flipped_psum[s][:])
        for s in range(SEQS):
            nc.tensor.matmul(result_psum[s][:], lhsT=values[:, s, :], rhs=flipped[:, s, :], start=True, stop=True)
        for s in range(SEQS):
            copy_out[s](result[:, spans[s]], result_psum[s][:])
            store[s](out[:, spans[s]], result[:, spans[s]])
